import numpy as np
import ml_dtypes


def mxq(x, axis, fmt="e4m3"):
    dtype, down = {"e4m3": (ml_dtypes.float8_e4m3fn, 7), "e5m2": (ml_dtypes.float8_e5m2, 14)}[fmt]
    v = np.moveaxis(np.asarray(x, np.float32).astype(ml_dtypes.bfloat16).astype(np.float64), axis, -1)
    blocks = v.reshape(v.shape[:-1] + (-1, 32))
    amax = np.abs(blocks).max(-1, keepdims=True)
    byte = np.maximum(np.where(amax > 0, np.frexp(amax)[1] - 1 + 127, 0) - down, 1)
    scale = np.exp2(byte - 127.0)
    codes = (blocks / scale).astype(np.float32).astype(dtype).astype(np.float64)
    return np.moveaxis((codes * scale).reshape(v.shape), -1, axis)


WIDE = False


def mx_kscale(k):
    if not WIDE:
        return np.ones(k)
    levels = np.array([10, -10, 5, -5, 0])
    a = np.random.permutation(np.resize(levels, k // 512 * 4)).reshape(k // 512, 4)
    idx = np.arange(k)
    return np.exp2(a[idx // 512, idx % 128 // 32])


BF16 = ml_dtypes.bfloat16


def bf(x):
    return np.asarray(x, np.float32).astype(BF16)


def f64(x):
    return np.asarray(x).astype(np.float64)


E2M1 = np.array([0.0, 0.5, 1.0, 1.5, 2.0, 3.0, 4.0, 6.0, -0.0, -0.5, -1.0, -1.5, -2.0, -3.0, -4.0, -6.0])


def pack_weight(w, fmt):
    k, n = w.shape
    w = f64(bf(w)).reshape(k // 32, 32, n)
    amax = np.abs(w).max(1)
    if fmt == "e4m3":
        byte = np.frexp(amax)[1] - 1 + 127 - 7
    else:
        mant, ex = np.frexp(amax / 6.0)
        byte = np.where(mant > 0.5, ex, ex - 1) + 127
    byte = np.clip(np.where(amax > 0, byte, 1), 1, 254)
    scaled = (w * np.exp2(127.0 - byte)[:, None, :]).reshape(k, n).astype(np.float32)
    by_word = np.ascontiguousarray(scaled.reshape(k // 512, 128, 4, n).transpose(0, 1, 3, 2))
    if fmt == "e4m3":
        words = by_word.astype(ml_dtypes.float8_e4m3fn).view(np.uint8)
    else:
        c = by_word.astype(ml_dtypes.float4_e2m1fn).view(np.uint8) & 0xF
        words = c[..., 0::2] | (c[..., 1::2] << 4)
    return np.ascontiguousarray(words), np.ascontiguousarray(byte.astype(np.uint8).reshape(k // 512, 16, n))


def unpack_weight(words, scales, fmt):
    g, p, n, _ = words.shape
    if fmt == "e4m3":
        vals = np.ascontiguousarray(words).view(ml_dtypes.float8_e4m3fn).astype(np.float64)
    else:
        nib = np.empty((g, p, n, 4), np.uint8)
        nib[..., 0::2] = words & 0xF
        nib[..., 1::2] = words >> 4
        vals = E2M1[nib]
    vals = vals * np.repeat(np.exp2(scales.astype(np.float64) - 127.0), 8, axis=1)[..., None]
    return vals.transpose(0, 1, 3, 2).reshape(g * 512, n)


NB, C, O, CZ, DD, HH, WW, MG = 1, 4096, 4096, 256, 2, 2, 4, 4
STRIDES = (2, 2, 2)
FMT = "e4m3"


def setup_inputs():
    s = mx_kscale(C)
    sd, sh, sw = STRIDES
    x = bf(np.random.standard_normal((NB, C, DD, HH, WW)) * s[None, :, None, None, None])
    z = bf(np.random.standard_normal((NB, CZ, sd * DD + MG, sh * HH + MG, sw * WW + MG)))
    w_oc = np.random.standard_normal((O, C)) / np.sqrt(C) / s[None, :]
    words, scales = pack_weight(np.ascontiguousarray(w_oc.T), FMT)
    b = bf(np.random.standard_normal(O) * 0.5)
    return {"x": x, "z": z, "W_words": words, "W_scales": scales, "b": b}


def reference(x, z, W_words, W_scales, b):
    sd, sh, sw = STRIDES
    u = np.repeat(np.repeat(np.repeat(f64(x), sd, axis=2), sh, axis=3), sw, axis=4)
    n, c, d, h, w = u.shape
    y = unpack_weight(W_words, W_scales, FMT).T @ mxq(u.reshape(n, c, d * h * w), 1, "e4m3")
    y = y.reshape(n, -1, d, h, w) + f64(b)[None, :, None, None, None]
    zf = f64(z)
    off = [(zf.shape[i] - y.shape[i]) // 2 for i in range(2, 5)]
    zc = zf[:, :,
            off[0]:off[0] + y.shape[2],
            off[1]:off[1] + y.shape[3],
            off[2]:off[2] + y.shape[4]]
    return np.concatenate([y, zc], axis=1)

@@ -1,0 +1,168 @@
+from contextlib import ExitStack
+
+import concourse.mybir as mybir
+from concourse.masks import make_identity
+
+BF16 = mybir.dt.bfloat16
+F32 = mybir.dt.float32
+I32 = mybir.dt.int32
+U32 = mybir.dt.uint32
+U8 = mybir.dt.uint8
+FP8X4 = mybir.dt.float8_e4m3fn_x4
+
+P = 128
+PACK = 4
+K_PASS = P * PACK
+C_IN = 4096
+C_OUT = 4096
+C_Z = 256
+PASSES = C_IN // K_PASS
+SRC_POS = 2 * 2 * 4
+POS = 4 * 4 * 8
+M_TILE = 128
+BANKS = 8
+ROUND_COLS = BANKS * M_TILE
+ROUNDS = C_OUT // ROUND_COLS
+LOAD_COLS = 1024
+PLANES_PER_TILE = 4
+QUADRANTS = 4
+
+FLOPS = 2 * C_IN * C_OUT * POS
+
+
+def tile_upconvcropcat_w_kernel(tc, x, z, W_words, W_scales, b, out):
+    nc = tc.nc
+    out_rows = out[0].rearrange("c i j k -> c (i j k)")
+
+    with ExitStack() as ctx:
+        keep = ctx.enter_context(tc.tile_pool(name="keep", bufs=1))
+        psum = ctx.enter_context(tc.psum_pool(name="psum", bufs=BANKS))
+        ctx.enter_context(tc.manual_schedule())
+
+        x_raw = keep.tile([P, PASSES, PACK, SRC_POS], BF16)
+        nc.sync.dma_start(
+            out=x_raw[:].rearrange("p g t s -> p g (t s)"),
+            in_=x[0].rearrange("(g p t) d h w -> p g (t d h w)", g=PASSES, p=P, t=PACK),
+        )
+        b_rows = keep.tile([P, P], BF16)
+        nc.gpsimd.memset(b_rows[:], 0.0)
+        nc.sync.dma_start(out=b_rows[0 : C_OUT // P, :], in_=b.rearrange("(j m) -> j m", m=P))
+        z_sb = keep.tile([P, 2, 4 * 8 * 12], BF16)
+        nc.sync.dma_start(
+            out=z_sb[:],
+            in_=z[0].rearrange("(p e) d h w -> p e (d h w)", e=2)[:, :, 2 * 96 : 6 * 96],
+        )
+
+        planes = keep.tile([P, PASSES // PLANES_PER_TILE, C_OUT], U8, align_bytes=64)
+        nc.vector.memset(planes[:].bitcast(I32), 0)
+        for a in range(PASSES // PLANES_PER_TILE):
+            for quad in range(QUADRANTS):
+                nc.sync.dma_start(
+                    out=planes[32 * quad : 32 * quad + 16, a, :].bitcast(I32),
+                    in_=W_scales[
+                        PLANES_PER_TILE * a : PLANES_PER_TILE * (a + 1), 4 * quad : 4 * quad + 4, :
+                    ].bitcast(I32),
+                )
+
+        w_words = {}
+        for c in range(C_OUT // LOAD_COLS):
+            for g in range(PASSES):
+                w_tile = keep.tile([P, LOAD_COLS], U32, name="w_%d_%d" % (c, g), align_bytes=64)
+                nc.sync.dma_start(
+                    out=w_tile[:].bitcast(I32),
+                    in_=W_words[g]
+                    .rearrange("p n t -> p (n t)")[:, PACK * LOAD_COLS * c : PACK * LOAD_COLS * (c + 1)]
+                    .bitcast(I32),
+                )
+                w_words[(c, g)] = w_tile
+
+        x_grouped = keep.tile([P, PASSES, SRC_POS, PACK], BF16)
+        nc.vector.tensor_copy(out=x_grouped[:], in_=x_raw[:].rearrange("p g t s -> p g s t"))
+        wide = keep.tile([P, PASSES * SRC_POS, 2, PACK], BF16)
+        nc.vector.tensor_copy(
+            out=wide[:],
+            in_=x_grouped[:]
+            .rearrange("p g s t -> p (g s) t")
+            .unsqueeze(2)
+            .to_broadcast([P, PASSES * SRC_POS, 2, PACK]),
+        )
+        tall = keep.tile([P, PASSES * 4, 2, 32], BF16)
+        nc.vector.tensor_copy(
+            out=tall[:],
+            in_=wide[:]
+            .rearrange("p (m w) c t -> p m (w c t)", w=4)
+            .unsqueeze(2)
+            .to_broadcast([P, PASSES * 4, 2, 32]),
+        )
+        u_bf = keep.tile([P, PASSES * 2, 2, 128], BF16, align_bytes=64)
+        nc.vector.tensor_copy(
+            out=u_bf[:],
+            in_=tall[:]
+            .rearrange("p (m h) b f -> p m (h b f)", h=2)
+            .unsqueeze(2)
+            .to_broadcast([P, PASSES * 2, 2, 128]),
+        )
+        u_codes = keep.tile([P, PASSES * POS], U32, align_bytes=64)
+        u_scales = keep.tile([P, PASSES * POS], U8, align_bytes=64)
+        nc.vector.quantize_mx(
+            out=u_codes[:].bitcast(FP8X4),
+            scales=u_scales[:],
+            in_=u_bf[:].rearrange("p m a f -> p (m a f)"),
+        )
+
+        ident = keep.tile([P, P], BF16)
+        make_identity(nc, ident[:])
+        b_cols_ps = psum.tile([P, P], BF16, tag="bank")
+        nc.tensor.transpose(b_cols_ps[:], b_rows[:], ident[:])
+        bias = keep.tile([P, C_OUT // P], F32)
+        nc.vector.tensor_copy(out=bias[:], in_=b_cols_ps[:, 0 : C_OUT // P])
+
+        zc = keep.tile([P, 2, POS], F32)
+        nc.scalar.copy(
+            out=zc[:].rearrange("p e (i j k) -> p (e i) j k", i=4, j=4, k=8),
+            in_=z_sb[:].rearrange("p e (i j k) -> p (e i) j k", i=4, j=8, k=12)[:, :, 2:6, 2:10],
+        )
+        nc.sync.dma_start(
+            out=out_rows[C_OUT : C_OUT + C_Z, :].rearrange("(p e) s -> p e s", e=2), in_=zc[:]
+        )
+
+        for r in range(ROUNDS):
+            accs = [psum.tile([P, POS], F32, name="acc_%d_%d" % (r, j), tag="bank") for j in range(BANKS)]
+            for g in range(PASSES):
+                plane_start = 4 * (g % PLANES_PER_TILE)
+                for j in range(BANKS):
+                    n0 = ROUND_COLS * r + M_TILE * j
+                    w_tile = w_words[(n0 // LOAD_COLS, g)]
+                    w0 = n0 % LOAD_COLS
+                    nc.tensor.matmul_mx(
+                        out=accs[j][:],
+                        lhsT=w_tile[:, w0 : w0 + M_TILE].bitcast(FP8X4),
+                        lhsT_scale=planes[plane_start:P, g // PLANES_PER_TILE, n0 : n0 + M_TILE],
+                        rhs=u_codes[:, POS * g : POS * (g + 1)].bitcast(FP8X4),
+                        rhs_scale=u_scales[:, POS * g : POS * (g + 1)],
+                        start=(g == 0),
+                        stop=(g == PASSES - 1),
+                    )
+            y_sb = keep.tile([P, BANKS, POS], F32, name="y_%d" % r)
+            for j in range(BANKS):
+                col = BANKS * r + j
+                if j % 2 == 0:
+                    nc.scalar.activation(
+                        out=y_sb[:, j, :],
+                        in_=accs[j][:],
+                        func=mybir.ActivationFunctionType.Identity,
+                        bias=bias[:, col : col + 1],
+                        scale=1.0,
+                    )
+                else:
+                    nc.vector.tensor_scalar(
+                        out=y_sb[:, j, :],
+                        in0=accs[j][:],
+                        scalar1=bias[:, col : col + 1],
+                        scalar2=None,
+                        op0=mybir.AluOpType.add,
+                    )
+            nc.sync.dma_start(
+                out=out_rows[ROUND_COLS * r : ROUND_COLS * (r + 1), :].rearrange("(j p) s -> p j s", p=P),
+                in_=y_sb[:],
+            )

@@ -57,11 +57,11 @@ def tile_upconvcropcat_w_kernel(tc, x, z, W_words, W_scales, b, out):
         nc.vector.memset(planes[:].bitcast(I32), 0)
         for a in range(PASSES // PLANES_PER_TILE):
             for quad in range(QUADRANTS):
-                nc.sync.dma_start(
-                    out=planes[32 * quad : 32 * quad + 16, a, :].bitcast(I32),
+                nc.gpsimd.dma_start(
+                    out=planes[32 * quad : 32 * quad + 16, a, :].bitcast(F32),
                     in_=W_scales[
                         PLANES_PER_TILE * a : PLANES_PER_TILE * (a + 1), 4 * quad : 4 * quad + 4, :
-                    ].bitcast(I32),
+                    ].bitcast(F32),
                 )
 
         w_words = {}

@@ -57,7 +57,8 @@ def tile_upconvcropcat_w_kernel(tc, x, z, W_words, W_scales, b, out):
         nc.vector.memset(planes[:].bitcast(I32), 0)
         for a in range(PASSES // PLANES_PER_TILE):
             for quad in range(QUADRANTS):
-                nc.gpsimd.dma_start(
+                queue = nc.scalar if quad < QUADRANTS // 2 else nc.gpsimd
+                queue.dma_start(
                     out=planes[32 * quad : 32 * quad + 16, a, :].bitcast(F32),
                     in_=W_scales[
                         PLANES_PER_TILE * a : PLANES_PER_TILE * (a + 1), 4 * quad : 4 * quad + 4, :

from contextlib import ExitStack

import concourse.mybir as mybir
from concourse.masks import make_identity

BF16 = mybir.dt.bfloat16
F32 = mybir.dt.float32
I32 = mybir.dt.int32
U32 = mybir.dt.uint32
U8 = mybir.dt.uint8
FP8X4 = mybir.dt.float8_e4m3fn_x4

P = 128
PACK = 4
K_PASS = P * PACK
C_IN = 4096
C_OUT = 4096
C_Z = 256
PASSES = C_IN // K_PASS
SRC_POS = 2 * 2 * 4
POS = 4 * 4 * 8
M_TILE = 128
BANKS = 8
ROUND_COLS = BANKS * M_TILE
ROUNDS = C_OUT // ROUND_COLS
LOAD_COLS = 1024
PLANES_PER_TILE = 4
QUADRANTS = 4

FLOPS = 2 * C_IN * C_OUT * POS


def tile_upconvcropcat_w_kernel(tc, x, z, W_words, W_scales, b, out):
    nc = tc.nc
    out_rows = out[0].rearrange("c i j k -> c (i j k)")

    with ExitStack() as ctx:
        keep = ctx.enter_context(tc.tile_pool(name="keep", bufs=1))
        psum = ctx.enter_context(tc.psum_pool(name="psum", bufs=BANKS))
        ctx.enter_context(tc.manual_schedule())

        x_raw = keep.tile([P, PASSES, PACK, SRC_POS], BF16)
        nc.sync.dma_start(
            out=x_raw[:].rearrange("p g t s -> p g (t s)"),
            in_=x[0].rearrange("(g p t) d h w -> p g (t d h w)", g=PASSES, p=P, t=PACK),
        )
        b_rows = keep.tile([P, P], BF16)
        nc.gpsimd.memset(b_rows[:], 0.0)
        nc.sync.dma_start(out=b_rows[0 : C_OUT // P, :], in_=b.rearrange("(j m) -> j m", m=P))
        z_sb = keep.tile([P, 2, 4 * 8 * 12], BF16)
        nc.sync.dma_start(
            out=z_sb[:],
            in_=z[0].rearrange("(p e) d h w -> p e (d h w)", e=2)[:, :, 2 * 96 : 6 * 96],
        )

        planes = keep.tile([P, PASSES // PLANES_PER_TILE, C_OUT], U8, align_bytes=64)
        nc.vector.memset(planes[:].bitcast(I32), 0)
        for a in range(PASSES // PLANES_PER_TILE):
            for quad in range(QUADRANTS):
                queue = nc.scalar if quad < QUADRANTS // 2 else nc.gpsimd
                queue.dma_start(
                    out=planes[32 * quad : 32 * quad + 16, a, :].bitcast(F32),
                    in_=W_scales[
                        PLANES_PER_TILE * a : PLANES_PER_TILE * (a + 1), 4 * quad : 4 * quad + 4, :
                    ].bitcast(F32),
                )

        w_words = {}
        for c in range(C_OUT // LOAD_COLS):
            for g in range(PASSES):
                w_tile = keep.tile([P, LOAD_COLS], U32, name="w_%d_%d" % (c, g), align_bytes=64)
                nc.sync.dma_start(
                    out=w_tile[:].bitcast(I32),
                    in_=W_words[g]
                    .rearrange("p n t -> p (n t)")[:, PACK * LOAD_COLS * c : PACK * LOAD_COLS * (c + 1)]
                    .bitcast(I32),
                )
                w_words[(c, g)] = w_tile

        x_grouped = keep.tile([P, PASSES, SRC_POS, PACK], BF16)
        nc.vector.tensor_copy(out=x_grouped[:], in_=x_raw[:].rearrange("p g t s -> p g s t"))
        wide = keep.tile([P, PASSES * SRC_POS, 2, PACK], BF16)
        nc.vector.tensor_copy(
            out=wide[:],
            in_=x_grouped[:]
            .rearrange("p g s t -> p (g s) t")
            .unsqueeze(2)
            .to_broadcast([P, PASSES * SRC_POS, 2, PACK]),
        )
        tall = keep.tile([P, PASSES * 4, 2, 32], BF16)
        nc.vector.tensor_copy(
            out=tall[:],
            in_=wide[:]
            .rearrange("p (m w) c t -> p m (w c t)", w=4)
            .unsqueeze(2)
            .to_broadcast([P, PASSES * 4, 2, 32]),
        )
        u_bf = keep.tile([P, PASSES * 2, 2, 128], BF16, align_bytes=64)
        nc.vector.tensor_copy(
            out=u_bf[:],
            in_=tall[:]
            .rearrange("p (m h) b f -> p m (h b f)", h=2)
            .unsqueeze(2)
            .to_broadcast([P, PASSES * 2, 2, 128]),
        )
        u_codes = keep.tile([P, PASSES * POS], U32, align_bytes=64)
        u_scales = keep.tile([P, PASSES * POS], U8, align_bytes=64)
        nc.vector.quantize_mx(
            out=u_codes[:].bitcast(FP8X4),
            scales=u_scales[:],
            in_=u_bf[:].rearrange("p m a f -> p (m a f)"),
        )

        ident = keep.tile([P, P], BF16)
        make_identity(nc, ident[:])
        b_cols_ps = psum.tile([P, P], BF16, tag="bank")
        nc.tensor.transpose(b_cols_ps[:], b_rows[:], ident[:])
        bias = keep.tile([P, C_OUT // P], F32)
        nc.vector.tensor_copy(out=bias[:], in_=b_cols_ps[:, 0 : C_OUT // P])

        zc = keep.tile([P, 2, POS], F32)
        nc.scalar.copy(
            out=zc[:].rearrange("p e (i j k) -> p (e i) j k", i=4, j=4, k=8),
            in_=z_sb[:].rearrange("p e (i j k) -> p (e i) j k", i=4, j=8, k=12)[:, :, 2:6, 2:10],
        )
        nc.sync.dma_start(
            out=out_rows[C_OUT : C_OUT + C_Z, :].rearrange("(p e) s -> p e s", e=2), in_=zc[:]
        )

        for r in range(ROUNDS):
            accs = [psum.tile([P, POS], F32, name="acc_%d_%d" % (r, j), tag="bank") for j in range(BANKS)]
            for g in range(PASSES):
                plane_start = 4 * (g % PLANES_PER_TILE)
                for j in range(BANKS):
                    n0 = ROUND_COLS * r + M_TILE * j
                    w_tile = w_words[(n0 // LOAD_COLS, g)]
                    w0 = n0 % LOAD_COLS
                    nc.tensor.matmul_mx(
                        out=accs[j][:],
                        lhsT=w_tile[:, w0 : w0 + M_TILE].bitcast(FP8X4),
                        lhsT_scale=planes[plane_start:P, g // PLANES_PER_TILE, n0 : n0 + M_TILE],
                        rhs=u_codes[:, POS * g : POS * (g + 1)].bitcast(FP8X4),
                        rhs_scale=u_scales[:, POS * g : POS * (g + 1)],
                        start=(g == 0),
                        stop=(g == PASSES - 1),
                    )
            y_sb = keep.tile([P, BANKS, POS], F32, name="y_%d" % r)
            for j in range(BANKS):
                col = BANKS * r + j
                if j % 2 == 0:
                    nc.scalar.activation(
                        out=y_sb[:, j, :],
                        in_=accs[j][:],
                        func=mybir.ActivationFunctionType.Identity,
                        bias=bias[:, col : col + 1],
                        scale=1.0,
                    )
                else:
                    nc.vector.tensor_scalar(
                        out=y_sb[:, j, :],
                        in0=accs[j][:],
                        scalar1=bias[:, col : col + 1],
                        scalar2=None,
                        op0=mybir.AluOpType.add,
                    )
            nc.sync.dma_start(
                out=out_rows[ROUND_COLS * r : ROUND_COLS * (r + 1), :].rearrange("(j p) s -> p j s", p=P),
                in_=y_sb[:],
            )
